import numpy as np
import ml_dtypes


def mxq(x, axis, fmt="e4m3"):
    dtype, down = {"e4m3": (ml_dtypes.float8_e4m3fn, 7), "e5m2": (ml_dtypes.float8_e5m2, 14)}[fmt]
    v = np.moveaxis(np.asarray(x, np.float32).astype(ml_dtypes.bfloat16).astype(np.float64), axis, -1)
    blocks = v.reshape(v.shape[:-1] + (-1, 32))
    amax = np.abs(blocks).max(-1, keepdims=True)
    byte = np.maximum(np.where(amax > 0, np.frexp(amax)[1] - 1 + 127, 0) - down, 1)
    scale = np.exp2(byte - 127.0)
    codes = (blocks / scale).astype(np.float32).astype(dtype).astype(np.float64)
    return np.moveaxis((codes * scale).reshape(v.shape), -1, axis)


WIDE = False


def mx_kscale(k):
    if not WIDE:
        return np.ones(k)
    levels = np.array([10, -10, 5, -5, 0])
    if k % 512:
        return np.exp2(np.random.permutation(np.resize(levels, k // 32))).repeat(32)
    a = np.empty((k // 512, 16))
    for p in range(k // 512):
        a[p, :8] = np.random.permutation(np.resize(levels, 8))
        for g in range(8):
            far = levels[np.abs(levels - a[p, g]) >= 10]
            a[p, g + 8] = far[np.random.randint(len(far))]
    return np.exp2(a.ravel()).repeat(32)


BF16 = ml_dtypes.bfloat16


def bf(x):
    return np.asarray(x, np.float32).astype(BF16)


def f64(x):
    return np.asarray(x).astype(np.float64)


B, N, D, DO, H, HID = 64, 128, 512, 256, 8, 2048


def setup_inputs():
    s, t = mx_kscale(D), mx_kscale(D)
    adj = np.random.uniform(size=(N, N))
    adj = adj / adj.sum(-1, keepdims=True)
    return {
        "h_norm": bf(np.random.standard_normal((B, N, D)) * s),
        "o_attn": bf(np.random.standard_normal((B, N, D)) * 0.25 * t),
        "a_gcn": bf(adj + np.random.standard_normal((N, N)) * 0.5 / np.sqrt(N)),
        "w_proj": bf(np.random.standard_normal((D, DO)) * 2.0 / np.sqrt(D) / t[:, None]),
        "b_proj": bf(np.random.standard_normal(DO) * 0.1),
        "gcn_w": bf(np.random.standard_normal((D, DO)) / np.sqrt(D) / s[:, None]),
        "gcn_m": bf(1.0 + 0.1 * np.random.standard_normal(DO)),
    }


def reference(h_norm, o_attn, a_gcn, w_proj, b_proj, gcn_w, gcn_m):
    o = (mxq(f64(o_attn), 2, "e4m3") @ mxq(f64(w_proj), 0, "e4m3")) + f64(b_proj)
    agg = f64(a_gcn) @ f64(h_norm)
    g = (mxq(agg, 2, "e4m3") @ mxq(f64(gcn_w), 0, "e4m3")) * f64(gcn_m)
    return o + g

@@ -1,0 +1,205 @@
+from contextlib import ExitStack
+
+import concourse.masks as masks
+import concourse.mybir as mybir
+
+F32 = mybir.dt.float32
+BF16 = mybir.dt.bfloat16
+U32 = mybir.dt.uint32
+U8 = mybir.dt.uint8
+FP8X4 = mybir.dt.float8_e4m3fn_x4
+MULT = mybir.AluOpType.mult
+ADD = mybir.AluOpType.add
+
+P = 128
+B, N, D, DO = 64, 128, 512, 256
+T = 4
+NBLK = B // T
+LEAD = 8
+VECTOR_COPIES = ((0, 1), (0, 3), (0, 5), (1, 4))
+FLOPS = 2 * 2 * B * N * D * DO + 2 * B * N * N * D
+
+
+def tile_gatblock_pa_t_kernel(tc, h_norm, o_attn, a_gcn, w_proj, b_proj, gcn_w, gcn_m, out):
+    nc = tc.nc
+    o_blk = o_attn.flatten_outer_dims().rearrange("(k p j) d -> k p (j d)", p=P, j=T)
+    out_blk = out.flatten_outer_dims().rearrange("(k p j) c -> k p (j c)", p=P, j=T)
+    h_blk = h_norm.rearrange("(k b) n d -> k n b d", b=T)
+
+    with ExitStack() as ctx:
+        consts = ctx.enter_context(tc.tile_pool(name="consts", bufs=1))
+        inputs = ctx.enter_context(tc.tile_pool(name="inputs", bufs=LEAD + 2))
+        work = ctx.enter_context(tc.tile_pool(name="work", bufs=3))
+        outs = ctx.enter_context(tc.tile_pool(name="outs", bufs=8))
+        ps_a = ctx.enter_context(tc.psum_pool(name="ps_a", bufs=4))
+        ps_m = ctx.enter_context(tc.psum_pool(name="ps_m", bufs=1))
+        ctx.enter_context(tc.manual_schedule())
+
+        o_tiles, h_tiles, grp_tiles, code_tiles, scale_tiles = {}, {}, {}, {}, {}
+        acc_tiles, res_tiles = {}, {}
+
+        def load(k, pieces):
+            o_sb = inputs.tile([P, T * D], BF16)
+            h_sb = inputs.tile([P, T, D], BF16)
+            o_tiles[k] = o_sb
+            h_tiles[k] = h_sb
+            wo = T * D // pieces
+            for q in range(pieces):
+                nc.sync.dma_start(out=o_sb[:, q * wo : (q + 1) * wo], in_=o_blk[k][:, q * wo : (q + 1) * wo])
+            wh = T // pieces
+            for q in range(pieces):
+                nc.sync.dma_start(out=h_sb[:, q * wh : (q + 1) * wh, :], in_=h_blk[k][:, q * wh : (q + 1) * wh, :])
+
+        a_sb = consts.tile([P, P], BF16)
+        nc.sync.dma_start(out=a_sb[:], in_=a_gcn)
+        vec_rows = consts.tile([P, 2 * DO], BF16)
+        nc.vector.memset(vec_rows[:], 0.0)
+        nc.sync.dma_start(out=vec_rows[0:1, 0:DO], in_=gcn_m.rearrange("(o c) -> o c", o=1))
+        nc.sync.dma_start(out=vec_rows[0:1, DO : 2 * DO], in_=b_proj.rearrange("(o c) -> o c", o=1))
+        w_raw = consts.tile([P, 2, 4, DO], BF16)
+        for w, w_hbm in ((1, gcn_w), (0, w_proj)):
+            nc.sync.dma_start(
+                out=w_raw[:, w, :, :].rearrange("p t c -> p (t c)"),
+                in_=w_hbm.rearrange("(p t) c -> p (t c)", t=4),
+            )
+        load(0, 2)
+        for k in range(1, LEAD):
+            load(k, 1)
+
+        ident = consts.tile([P, P], F32)
+        masks.make_identity(nc, ident[:])
+        ones = consts.tile([P, P], BF16)
+        nc.vector.memset(ones[:], 1.0)
+        ident_bf = consts.tile([P, P], BF16)
+        nc.vector.tensor_copy(out=ident_bf[:], in_=ident[:])
+        at_ps = ps_a.tile([P, P], BF16, tag="a")
+        nc.tensor.transpose(at_ps[:], a_sb[:], ident_bf[:])
+        a_t = consts.tile([P, P], BF16)
+        nc.vector.tensor_copy(out=a_t[:], in_=at_ps[:])
+
+        m_bc = consts.tile([P, 2, DO], F32)
+        b_bc = consts.tile([P, 2, DO], F32)
+        vec_ps = ps_a.tile([P, 2 * DO], F32, tag="a")
+        nc.tensor.matmul(vec_ps[:], lhsT=ones[:], rhs=vec_rows[:], start=True, stop=True)
+        for r in range(2):
+            nc.scalar.copy(out=m_bc[:, r, :], in_=vec_ps[:, 0:DO])
+            nc.scalar.copy(out=b_bc[:, r, :], in_=vec_ps[:, DO : 2 * DO])
+
+        w_grp = consts.tile([P, 2, DO, 4], BF16, align_bytes=64)
+        w_codes = consts.tile([P, 2 * DO], U32, align_bytes=64)
+        w_scales = consts.tile([P, 2 * DO], U8, align_bytes=64)
+        for w in (1, 0):
+            nc.vector.tensor_copy(out=w_grp[:, w, :, :], in_=w_raw[:, w, :, :].rearrange("p t c -> p c t"))
+        nc.vector.quantize_mx(
+            out=w_codes[:].bitcast(FP8X4), scales=w_scales[:], in_=w_grp[:].rearrange("p w c t -> p (w c t)")
+        )
+
+        def copy_out(i, bank, dst, src):
+            if (i, bank) in VECTOR_COPIES:
+                nc.vector.tensor_copy(out=dst, in_=src)
+            else:
+                nc.scalar.copy(out=dst, in_=src)
+
+        def transposes(i):
+            o_words = o_tiles[i][:].bitcast(F32)
+            grp = work.tile([P, 2, T * P * 4], BF16, align_bytes=64)
+            grp_tiles[i] = grp
+            go_words = grp[:, 0, :].bitcast(F32).rearrange("p (j r u) -> p j r u", j=T, u=2)
+            for half in range(2):
+                xt = ps_a.tile([P, 2, 2, P], F32, tag="a")
+                for jj in range(2):
+                    for u in range(2):
+                        c0 = 256 * (2 * half + jj)
+                        nc.tensor.transpose(xt[:, jj, u, :], o_words[:, c0 + u : c0 + 256 : 2], ident[:])
+                copy_out(i, half, go_words[:, 2 * half : 2 * half + 2, :, :], xt[:].rearrange("p j u r -> p j r u"))
+
+        def mix(i, b):
+            ag = ps_a.tile([P, 4, P], F32, tag="a")
+            for t in range(4):
+                nc.tensor.matmul(
+                    ag[:, t, :], lhsT=h_tiles[i][:, b, t:D:4], rhs=a_t[:], start=True, stop=True
+                )
+            gg = grp_tiles[i][:, 1, :].rearrange("p (j r t) -> p j r t", j=T, t=4)
+            copy_out(i, 2 + b, gg[:, :, 32 * b : 32 * b + 32, :], ag[:].rearrange("p t (r j) -> p j r t", j=T))
+
+        def quantise(i):
+            codes = work.tile([P, 2 * T * P], U32, align_bytes=64)
+            scales = work.tile([P, 2 * T * P], U8, align_bytes=64)
+            nc.vector.quantize_mx(
+                out=codes[:].bitcast(FP8X4), scales=scales[:], in_=grp_tiles[i][:].rearrange("p w c -> p (w c)")
+            )
+            code_tiles[i] = codes
+            scale_tiles[i] = scales
+
+        def mx_passes(i, which, half):
+            acc = ps_m.tile([P, 2, DO], F32, tag="m%d%d" % (which, half))
+            acc_tiles[(i, which, half)] = acc
+            for jj in range(2):
+                c0 = T * P * which + P * (2 * half + jj)
+                nc.tensor.matmul_mx(
+                    out=acc[:, jj, :],
+                    lhsT=code_tiles[i][:, c0 : c0 + P].bitcast(FP8X4),
+                    lhsT_scale=scale_tiles[i][:, c0 : c0 + P],
+                    rhs=w_codes[:, DO * which : DO * which + DO].bitcast(FP8X4),
+                    rhs_scale=w_scales[:, DO * which : DO * which + DO],
+                    start=True,
+                    stop=True,
+                )
+
+        def scale_g(i, half):
+            if half == 0:
+                res = outs.tile([P, T, DO], F32)
+                res_tiles[i] = res
+            part = res_tiles[i][:, 2 * half : 2 * half + 2, :]
+            nc.vector.tensor_tensor(out=part, in0=acc_tiles[(i, 1, half)][:], in1=m_bc[:], op=MULT)
+
+        def add_o(i, half):
+            part = res_tiles[i][:, 2 * half : 2 * half + 2, :]
+            nc.vector.tensor_tensor(out=part, in0=acc_tiles[(i, 0, half)][:], in1=part, op=ADD)
+            if i == NBLK - 1 and half == 1:
+                nc.vector.tensor_tensor(out=part, in0=part, in1=b_bc[:], op=ADD)
+            else:
+                nc.gpsimd.tensor_tensor(out=part, in0=part, in1=b_bc[:], op=ADD)
+            if i == NBLK - 1:
+                c0 = 2 * half * DO
+                nc.sync.dma_start(
+                    out=out_blk[i][:, c0 : c0 + 2 * DO], in_=part.rearrange("p j c -> p (j c)")
+                )
+
+        def store(i):
+            nc.sync.dma_start(out=out_blk[i], in_=res_tiles[i][:].rearrange("p j c -> p (j c)"))
+
+        def live(i):
+            return 0 <= i < NBLK
+
+        for w in range(-2, NBLK + 1):
+            if live(w):
+                quantise(w)
+            if live(w - 2) and w - 2 < NBLK - 1:
+                store(w - 2)
+            if live(w + 1):
+                mix(w + 1, 2)
+            if live(w):
+                mx_passes(w, 1, 0)
+            if live(w + 1):
+                mix(w + 1, 3)
+            if live(w + 2):
+                transposes(w + 2)
+                mix(w + 2, 0)
+            if live(w - 1):
+                add_o(w - 1, 0)
+            if live(w):
+                mx_passes(w, 0, 0)
+            if live(w - 1):
+                scale_g(w - 1, 1)
+            if live(w):
+                mx_passes(w, 1, 1)
+                scale_g(w, 0)
+            if live(w - 1):
+                add_o(w - 1, 1)
+            if live(w):
+                mx_passes(w, 0, 1)
+            if live(w + 2):
+                mix(w + 2, 1)
+            if live(w + 2 + LEAD):
+                load(w + 2 + LEAD, 1)

@@ -13,22 +13,19 @@ ADD = mybir.AluOpType.add
 
 P = 128
 B, N, D, DO = 64, 128, 512, 256
-T = 4
-NBLK = B // T
-LEAD = 8
-VECTOR_COPIES = ((0, 1), (0, 3), (0, 5), (1, 4))
+TMAX = 4
+SIZES = (2, 2) + (4,) * 14 + (2, 2)
+STARTS = tuple(sum(SIZES[:i]) for i in range(len(SIZES)))
+NBLK = len(SIZES)
+LEAD = 10
 FLOPS = 2 * 2 * B * N * D * DO + 2 * B * N * N * D
 
 
 def tile_gatblock_pa_t_kernel(tc, h_norm, o_attn, a_gcn, w_proj, b_proj, gcn_w, gcn_m, out):
     nc = tc.nc
-    o_blk = o_attn.flatten_outer_dims().rearrange("(k p j) d -> k p (j d)", p=P, j=T)
-    out_blk = out.flatten_outer_dims().rearrange("(k p j) c -> k p (j c)", p=P, j=T)
-    h_blk = h_norm.rearrange("(k b) n d -> k n b d", b=T)
 
     with ExitStack() as ctx:
         consts = ctx.enter_context(tc.tile_pool(name="consts", bufs=1))
-        inputs = ctx.enter_context(tc.tile_pool(name="inputs", bufs=LEAD + 2))
         work = ctx.enter_context(tc.tile_pool(name="work", bufs=3))
         outs = ctx.enter_context(tc.tile_pool(name="outs", bufs=8))
         ps_a = ctx.enter_context(tc.psum_pool(name="ps_a", bufs=4))
@@ -38,33 +35,31 @@ def tile_gatblock_pa_t_kernel(tc, h_norm, o_attn, a_gcn, w_proj, b_proj, gcn_w, 
         o_tiles, h_tiles, grp_tiles, code_tiles, scale_tiles = {}, {}, {}, {}, {}
         acc_tiles, res_tiles = {}, {}
 
-        def load(k, pieces):
-            o_sb = inputs.tile([P, T * D], BF16)
-            h_sb = inputs.tile([P, T, D], BF16)
+        def load(k):
+            s0, n = STARTS[k], SIZES[k]
+            o_sb = consts.tile([P, n * D], BF16, name="o%d" % k)
+            h_sb = consts.tile([P, n, D], BF16, name="h%d" % k)
             o_tiles[k] = o_sb
             h_tiles[k] = h_sb
-            wo = T * D // pieces
-            for q in range(pieces):
-                nc.sync.dma_start(out=o_sb[:, q * wo : (q + 1) * wo], in_=o_blk[k][:, q * wo : (q + 1) * wo])
-            wh = T // pieces
-            for q in range(pieces):
-                nc.sync.dma_start(out=h_sb[:, q * wh : (q + 1) * wh, :], in_=h_blk[k][:, q * wh : (q + 1) * wh, :])
+            o_rows = o_attn[s0 : s0 + n, :, :].flatten_outer_dims()
+            nc.sync.dma_start(out=o_sb[:], in_=o_rows.rearrange("(p j) d -> p (j d)", p=P))
+            nc.sync.dma_start(out=h_sb[:], in_=h_norm[s0 : s0 + n, :, :].rearrange("b n d -> n b d"))
 
         a_sb = consts.tile([P, P], BF16)
         nc.sync.dma_start(out=a_sb[:], in_=a_gcn)
         vec_rows = consts.tile([P, 2 * DO], BF16)
         nc.vector.memset(vec_rows[:], 0.0)
-        nc.sync.dma_start(out=vec_rows[0:1, 0:DO], in_=gcn_m.rearrange("(o c) -> o c", o=1))
-        nc.sync.dma_start(out=vec_rows[0:1, DO : 2 * DO], in_=b_proj.rearrange("(o c) -> o c", o=1))
         w_raw = consts.tile([P, 2, 4, DO], BF16)
+        load(0)
         for w, w_hbm in ((1, gcn_w), (0, w_proj)):
             nc.sync.dma_start(
                 out=w_raw[:, w, :, :].rearrange("p t c -> p (t c)"),
                 in_=w_hbm.rearrange("(p t) c -> p (t c)", t=4),
             )
-        load(0, 2)
+        nc.sync.dma_start(out=vec_rows[0:1, 0:DO], in_=gcn_m.rearrange("(o c) -> o c", o=1))
+        nc.sync.dma_start(out=vec_rows[0:1, DO : 2 * DO], in_=b_proj.rearrange("(o c) -> o c", o=1))
         for k in range(1, LEAD):
-            load(k, 1)
+            load(k)
 
         ident = consts.tile([P, P], F32)
         masks.make_identity(nc, ident[:])
@@ -77,65 +72,93 @@ def tile_gatblock_pa_t_kernel(tc, h_norm, o_attn, a_gcn, w_proj, b_proj, gcn_w, 
         a_t = consts.tile([P, P], BF16)
         nc.vector.tensor_copy(out=a_t[:], in_=at_ps[:])
 
-        m_bc = consts.tile([P, 2, DO], F32)
-        b_bc = consts.tile([P, 2, DO], F32)
-        vec_ps = ps_a.tile([P, 2 * DO], F32, tag="a")
-        nc.tensor.matmul(vec_ps[:], lhsT=ones[:], rhs=vec_rows[:], start=True, stop=True)
-        for r in range(2):
-            nc.scalar.copy(out=m_bc[:, r, :], in_=vec_ps[:, 0:DO])
-            nc.scalar.copy(out=b_bc[:, r, :], in_=vec_ps[:, DO : 2 * DO])
-
         w_grp = consts.tile([P, 2, DO, 4], BF16, align_bytes=64)
         w_codes = consts.tile([P, 2 * DO], U32, align_bytes=64)
         w_scales = consts.tile([P, 2 * DO], U8, align_bytes=64)
-        for w in (1, 0):
-            nc.vector.tensor_copy(out=w_grp[:, w, :, :], in_=w_raw[:, w, :, :].rearrange("p t c -> p c t"))
-        nc.vector.quantize_mx(
-            out=w_codes[:].bitcast(FP8X4), scales=w_scales[:], in_=w_grp[:].rearrange("p w c t -> p (w c t)")
+        nc.gpsimd.tensor_scalar(
+            out=w_grp[:, 0, :, :], in0=w_raw[:, 0, :, :].rearrange("p t c -> p c t"),
+            scalar1=1.0, scalar2=0.0, op0=MULT, op1=ADD,
         )
+        nc.vector.tensor_copy(out=w_grp[:, 1, :, :], in_=w_raw[:, 1, :, :].rearrange("p t c -> p c t"))
 
-        def copy_out(i, bank, dst, src):
-            if (i, bank) in VECTOR_COPIES:
-                nc.vector.tensor_copy(out=dst, in_=src)
-            else:
-                nc.scalar.copy(out=dst, in_=src)
+        def quantise_weight(w):
+            cols = slice(DO * w, DO * w + DO)
+            nc.vector.quantize_mx(
+                out=w_codes[:, cols].bitcast(FP8X4),
+                scales=w_scales[:, cols],
+                in_=w_grp[:, w, :, :].rearrange("p c t -> p (c t)"),
+            )
 
-        def transposes(i):
-            o_words = o_tiles[i][:].bitcast(F32)
-            grp = work.tile([P, 2, T * P * 4], BF16, align_bytes=64)
+        m_bc = consts.tile([P, DO], F32)
+        b_bc = consts.tile([P, DO], F32)
+
+        def spread_vectors():
+            vec_ps = ps_a.tile([P, 2 * DO], F32, tag="a")
+            nc.tensor.matmul(vec_ps[:], lhsT=ones[:], rhs=vec_rows[:], start=True, stop=True)
+            nc.scalar.copy(out=m_bc[:], in_=vec_ps[:, 0:DO])
+            nc.scalar.copy(out=b_bc[:], in_=vec_ps[:, DO : 2 * DO])
+
+        def rows(vec, n):
+            return vec[:].unsqueeze(1).to_broadcast([P, n, DO])
+
+        def new_grp(i):
+            grp = work.tile([P, TMAX * P * 8], BF16, align_bytes=64)
             grp_tiles[i] = grp
-            go_words = grp[:, 0, :].bitcast(F32).rearrange("p (j r u) -> p j r u", j=T, u=2)
-            for half in range(2):
-                xt = ps_a.tile([P, 2, 2, P], F32, tag="a")
-                for jj in range(2):
-                    for u in range(2):
-                        c0 = 256 * (2 * half + jj)
-                        nc.tensor.transpose(xt[:, jj, u, :], o_words[:, c0 + u : c0 + 256 : 2], ident[:])
-                copy_out(i, half, go_words[:, 2 * half : 2 * half + 2, :, :], xt[:].rearrange("p j u r -> p j r u"))
+
+        def transposes(i, j0):
+            n = SIZES[i]
+            if j0 == 0:
+                new_grp(i)
+            nj = min(2, n - j0)
+            o_words = o_tiles[i][:].bitcast(F32)
+            go_words = grp_tiles[i][:, 0 : n * P * 4].bitcast(F32).rearrange("p (j r u) -> p j r u", j=n, u=2)
+            xt = ps_a.tile([P, 2, 2, P], F32, tag="a")
+            for jj in range(nj):
+                for u in range(2):
+                    c0 = 256 * (j0 + jj)
+                    nc.tensor.transpose(xt[:, jj, u, :], o_words[:, c0 + u : c0 + 256 : 2], ident[:])
+            nc.scalar.copy(out=go_words[:, j0 : j0 + nj, :, :], in_=xt[:, 0:nj, :, :].rearrange("p j u r -> p j r u"))
 
         def mix(i, b):
+            n = SIZES[i]
+            r = P // n
             ag = ps_a.tile([P, 4, P], F32, tag="a")
             for t in range(4):
-                nc.tensor.matmul(
-                    ag[:, t, :], lhsT=h_tiles[i][:, b, t:D:4], rhs=a_t[:], start=True, stop=True
-                )
-            gg = grp_tiles[i][:, 1, :].rearrange("p (j r t) -> p j r t", j=T, t=4)
-            copy_out(i, 2 + b, gg[:, :, 32 * b : 32 * b + 32, :], ag[:].rearrange("p t (r j) -> p j r t", j=T))
+                nc.tensor.matmul(ag[:, t, :], lhsT=h_tiles[i][:, b, t:D:4], rhs=a_t[:], start=True, stop=True)
+            gg = grp_tiles[i][:, n * P * 4 : n * P * 8].rearrange("p (j r t) -> p j r t", j=n, t=4)
+            copy = nc.vector.tensor_copy if i < 2 and b == n - 1 else nc.scalar.copy
+            copy(out=gg[:, :, r * b : r * b + r, :], in_=ag[:].rearrange("p t (r j) -> p j r t", j=n))
 
         def quantise(i):
-            codes = work.tile([P, 2 * T * P], U32, align_bytes=64)
-            scales = work.tile([P, 2 * T * P], U8, align_bytes=64)
+            n = SIZES[i]
+            codes = work.tile([P, 2 * TMAX * P], U32, align_bytes=64)
+            scales = work.tile([P, 2 * TMAX * P], U8, align_bytes=64)
             nc.vector.quantize_mx(
-                out=codes[:].bitcast(FP8X4), scales=scales[:], in_=grp_tiles[i][:].rearrange("p w c -> p (w c)")
+                out=codes[:, 0 : 2 * n * P].bitcast(FP8X4),
+                scales=scales[:, 0 : 2 * n * P],
+                in_=grp_tiles[i][:, 0 : n * P * 8],
             )
             code_tiles[i] = codes
             scale_tiles[i] = scales
 
+        def halves(i):
+            return (SIZES[i] + 1) // 2
+
+        single = {}
+        for i in range(NBLK):
+            single[i] = 1 - single[i - 1] if i > 0 and halves(i - 1) == 1 else 0
+
+        def bank(i, half):
+            return half if halves(i) == 2 else single[i]
+
+        def width(i):
+            return min(2, SIZES[i])
+
         def mx_passes(i, which, half):
-            acc = ps_m.tile([P, 2, DO], F32, tag="m%d%d" % (which, half))
+            acc = ps_m.tile([P, 2, DO], F32, tag="m%d%d" % (which, bank(i, half)))
             acc_tiles[(i, which, half)] = acc
-            for jj in range(2):
-                c0 = T * P * which + P * (2 * half + jj)
+            for jj in range(width(i)):
+                c0 = SIZES[i] * P * which + P * (2 * half + jj)
                 nc.tensor.matmul_mx(
                     out=acc[:, jj, :],
                     lhsT=code_tiles[i][:, c0 : c0 + P].bitcast(FP8X4),
@@ -148,58 +171,82 @@ def tile_gatblock_pa_t_kernel(tc, h_norm, o_attn, a_gcn, w_proj, b_proj, gcn_w, 
 
         def scale_g(i, half):
             if half == 0:
-                res = outs.tile([P, T, DO], F32)
+                res = outs.tile([P, TMAX, DO], F32)
                 res_tiles[i] = res
-            part = res_tiles[i][:, 2 * half : 2 * half + 2, :]
-            nc.vector.tensor_tensor(out=part, in0=acc_tiles[(i, 1, half)][:], in1=m_bc[:], op=MULT)
+            n = width(i)
+            part = res_tiles[i][:, 2 * half : 2 * half + n, :]
+            nc.vector.tensor_tensor(out=part, in0=acc_tiles[(i, 1, half)][:, 0:n, :], in1=rows(m_bc, n), op=MULT)
 
         def add_o(i, half):
-            part = res_tiles[i][:, 2 * half : 2 * half + 2, :]
-            nc.vector.tensor_tensor(out=part, in0=acc_tiles[(i, 0, half)][:], in1=part, op=ADD)
-            if i == NBLK - 1 and half == 1:
-                nc.vector.tensor_tensor(out=part, in0=part, in1=b_bc[:], op=ADD)
-            else:
-                nc.gpsimd.tensor_tensor(out=part, in0=part, in1=b_bc[:], op=ADD)
-            if i == NBLK - 1:
-                c0 = 2 * half * DO
-                nc.sync.dma_start(
-                    out=out_blk[i][:, c0 : c0 + 2 * DO], in_=part.rearrange("p j c -> p (j c)")
-                )
+            n = width(i)
+            part = res_tiles[i][:, 2 * half : 2 * half + n, :]
+            nc.vector.tensor_tensor(out=part, in0=acc_tiles[(i, 0, half)][:, 0:n, :], in1=part, op=ADD)
+            eng = nc.vector if i == NBLK - 1 else nc.gpsimd
+            eng.tensor_tensor(out=part, in0=part, in1=rows(b_bc, n), op=ADD)
 
         def store(i):
-            nc.sync.dma_start(out=out_blk[i], in_=res_tiles[i][:].rearrange("p j c -> p (j c)"))
+            s0, n = STARTS[i], SIZES[i]
+            out_rows = out[s0 : s0 + n, :, :].flatten_outer_dims()
+            nc.sync.dma_start(
+                out=out_rows.rearrange("(p j) c -> p (j c)", p=P),
+                in_=res_tiles[i][:, 0:n, :].rearrange("p j c -> p (j c)"),
+            )
 
         def live(i):
             return 0 <= i < NBLK
 
+        fill, ends, leads = [], [], []
+        for i in range(NBLK):
+            n = SIZES[i]
+            own = [("t", i, j) for j in range(0, n, 2)] + [("m", i, b) for b in range(n)]
+            leads.append(len(fill) + (2 * len(own) + 2) // 3)
+            fill += own
+            ends.append(len(fill))
+
+        def upto(w):
+            if w + 2 >= NBLK:
+                return len(fill)
+            return max(leads[w + 2] if w + 2 >= 0 else 0, ends[w + 1] if w + 1 >= 0 else 0)
+
+        def run_fill(items):
+            for kind, i, x in items:
+                if kind == "t":
+                    transposes(i, x)
+                else:
+                    mix(i, x)
+
         for w in range(-2, NBLK + 1):
+            todo = fill[(upto(w - 1) if w > -2 else 0) : upto(w)]
+            if w == 0:
+                quantise_weight(1)
             if live(w):
                 quantise(w)
-            if live(w - 2) and w - 2 < NBLK - 1:
+            if w == 0:
+                quantise_weight(0)
+            if live(w - 2):
                 store(w - 2)
-            if live(w + 1):
-                mix(w + 1, 2)
+            run_fill(todo[:1])
             if live(w):
                 mx_passes(w, 1, 0)
-            if live(w + 1):
-                mix(w + 1, 3)
-            if live(w + 2):
-                transposes(w + 2)
-                mix(w + 2, 0)
+            run_fill(todo[1:-1])
+            if w == -1:
+                spread_vectors()
             if live(w - 1):
                 add_o(w - 1, 0)
             if live(w):
                 mx_passes(w, 0, 0)
-            if live(w - 1):
+            if live(w - 1) and halves(w - 1) == 2:
                 scale_g(w - 1, 1)
-            if live(w):
+            if live(w) and halves(w) == 2:
                 mx_passes(w, 1, 1)
-                scale_g(w, 0)
-            if live(w - 1):
-                add_o(w - 1, 1)
             if live(w):
+                scale_g(w, 0)
+            if live(w - 1) and halves(w - 1) == 2:
+                add_o(w - 1, 1)
+            if live(w) and halves(w) == 2:
                 mx_passes(w, 0, 1)
-            if live(w + 2):
-                mix(w + 2, 1)
+            if len(todo) > 1:
+                run_fill(todo[-1:])
             if live(w + 2 + LEAD):
-                load(w + 2 + LEAD, 1)
+                load(w + 2 + LEAD)
+        store(NBLK - 1)

@@ -14,7 +14,7 @@ ADD = mybir.AluOpType.add
 P = 128
 B, N, D, DO = 64, 128, 512, 256
 TMAX = 4
-SIZES = (2, 2) + (4,) * 14 + (2, 2)
+SIZES = (4,) * 15 + (2, 2)
 STARTS = tuple(sum(SIZES[:i]) for i in range(len(SIZES)))
 NBLK = len(SIZES)
 LEAD = 10
@@ -42,8 +42,19 @@ def tile_gatblock_pa_t_kernel(tc, h_norm, o_attn, a_gcn, w_proj, b_proj, gcn_w, 
             o_tiles[k] = o_sb
             h_tiles[k] = h_sb
             o_rows = o_attn[s0 : s0 + n, :, :].flatten_outer_dims()
-            nc.sync.dma_start(out=o_sb[:], in_=o_rows.rearrange("(p j) d -> p (j d)", p=P))
-            nc.sync.dma_start(out=h_sb[:], in_=h_norm[s0 : s0 + n, :, :].rearrange("b n d -> n b d"))
+            pieces = 2 if k == 0 else 1
+            c = n * D // pieces
+            for q in range(pieces):
+                nc.sync.dma_start(
+                    out=o_sb[:, c * q : c * (q + 1)],
+                    in_=o_rows.rearrange("(p j) d -> p (j d)", p=P)[:, c * q : c * (q + 1)],
+                )
+            c = n // pieces
+            for q in range(pieces):
+                nc.sync.dma_start(
+                    out=h_sb[:, c * q : c * (q + 1), :],
+                    in_=h_norm[s0 + c * q : s0 + c * (q + 1), :, :].rearrange("b n d -> n b d"),
+                )
 
         a_sb = consts.tile([P, P], BF16)
         nc.sync.dma_start(out=a_sb[:], in_=a_gcn)
@@ -79,7 +90,6 @@ def tile_gatblock_pa_t_kernel(tc, h_norm, o_attn, a_gcn, w_proj, b_proj, gcn_w, 
             out=w_grp[:, 0, :, :], in0=w_raw[:, 0, :, :].rearrange("p t c -> p c t"),
             scalar1=1.0, scalar2=0.0, op0=MULT, op1=ADD,
         )
-        nc.vector.tensor_copy(out=w_grp[:, 1, :, :], in_=w_raw[:, 1, :, :].rearrange("p t c -> p c t"))
 
         def quantise_weight(w):
             cols = slice(DO * w, DO * w + DO)
@@ -126,7 +136,7 @@ def tile_gatblock_pa_t_kernel(tc, h_norm, o_attn, a_gcn, w_proj, b_proj, gcn_w, 
             for t in range(4):
                 nc.tensor.matmul(ag[:, t, :], lhsT=h_tiles[i][:, b, t:D:4], rhs=a_t[:], start=True, stop=True)
             gg = grp_tiles[i][:, n * P * 4 : n * P * 8].rearrange("p (j r t) -> p j r t", j=n, t=4)
-            copy = nc.vector.tensor_copy if i < 2 and b == n - 1 else nc.scalar.copy
+            copy = nc.vector.tensor_copy if i == 0 and b % 2 == 1 else nc.scalar.copy
             copy(out=gg[:, :, r * b : r * b + r, :], in_=ag[:].rearrange("p t (r j) -> p j r t", j=n))
 
         def quantise(i):
@@ -181,8 +191,12 @@ def tile_gatblock_pa_t_kernel(tc, h_norm, o_attn, a_gcn, w_proj, b_proj, gcn_w, 
             n = width(i)
             part = res_tiles[i][:, 2 * half : 2 * half + n, :]
             nc.vector.tensor_tensor(out=part, in0=acc_tiles[(i, 0, half)][:, 0:n, :], in1=part, op=ADD)
+
+        def add_bias(i):
+            n = SIZES[i]
+            res = res_tiles[i][:, 0:n, :]
             eng = nc.vector if i == NBLK - 1 else nc.gpsimd
-            eng.tensor_tensor(out=part, in0=part, in1=rows(b_bc, n), op=ADD)
+            eng.tensor_tensor(out=res, in0=res, in1=rows(b_bc, n), op=ADD)
 
         def store(i):
             s0, n = STARTS[i], SIZES[i]
@@ -217,11 +231,11 @@ def tile_gatblock_pa_t_kernel(tc, h_norm, o_attn, a_gcn, w_proj, b_proj, gcn_w, 
 
         for w in range(-2, NBLK + 1):
             todo = fill[(upto(w - 1) if w > -2 else 0) : upto(w)]
-            if w == 0:
-                quantise_weight(1)
             if live(w):
                 quantise(w)
             if w == 0:
+                nc.vector.tensor_copy(out=w_grp[:, 1, :, :], in_=w_raw[:, 1, :, :].rearrange("p t c -> p c t"))
+                quantise_weight(1)
                 quantise_weight(0)
             if live(w - 2):
                 store(w - 2)
@@ -233,6 +247,8 @@ def tile_gatblock_pa_t_kernel(tc, h_norm, o_attn, a_gcn, w_proj, b_proj, gcn_w, 
                 spread_vectors()
             if live(w - 1):
                 add_o(w - 1, 0)
+            if live(w - 1) and halves(w - 1) == 1:
+                add_bias(w - 1)
             if live(w):
                 mx_passes(w, 0, 0)
             if live(w - 1) and halves(w - 1) == 2:
@@ -243,6 +259,7 @@ def tile_gatblock_pa_t_kernel(tc, h_norm, o_attn, a_gcn, w_proj, b_proj, gcn_w, 
                 scale_g(w, 0)
             if live(w - 1) and halves(w - 1) == 2:
                 add_o(w - 1, 1)
+                add_bias(w - 1)
             if live(w) and halves(w) == 2:
                 mx_passes(w, 0, 1)
             if len(todo) > 1:

@@ -18,6 +18,7 @@ SIZES = (4,) * 15 + (2, 2)
 STARTS = tuple(sum(SIZES[:i]) for i in range(len(SIZES)))
 NBLK = len(SIZES)
 LEAD = 10
+WARM = 10
 FLOPS = 2 * 2 * B * N * D * DO + 2 * B * N * N * D
 
 
@@ -43,39 +44,42 @@ def tile_gatblock_pa_t_kernel(tc, h_norm, o_attn, a_gcn, w_proj, b_proj, gcn_w, 
             h_tiles[k] = h_sb
             o_rows = o_attn[s0 : s0 + n, :, :].flatten_outer_dims()
             pieces = 2 if k == 0 else 1
-            c = n * D // pieces
-            for q in range(pieces):
-                nc.sync.dma_start(
-                    out=o_sb[:, c * q : c * (q + 1)],
-                    in_=o_rows.rearrange("(p j) d -> p (j d)", p=P)[:, c * q : c * (q + 1)],
-                )
             c = n // pieces
             for q in range(pieces):
                 nc.sync.dma_start(
                     out=h_sb[:, c * q : c * (q + 1), :],
                     in_=h_norm[s0 + c * q : s0 + c * (q + 1), :, :].rearrange("b n d -> n b d"),
                 )
+            c = n * D // pieces
+            for q in range(pieces):
+                nc.sync.dma_start(
+                    out=o_sb[:, c * q : c * (q + 1)],
+                    in_=o_rows.rearrange("(p j) d -> p (j d)", p=P)[:, c * q : c * (q + 1)],
+                )
 
+        ones = consts.tile([P, P], BF16)
+        nc.vector.memset(ones[:], 1.0)
+        warm_ps = ps_a.tile([P, P], F32, tag="a")
+        for x in range(WARM):
+            nc.tensor.matmul(warm_ps[:], lhsT=ones[:], rhs=ones[:], start=True, stop=True)
         a_sb = consts.tile([P, P], BF16)
         nc.sync.dma_start(out=a_sb[:], in_=a_gcn)
         vec_rows = consts.tile([P, 2 * DO], BF16)
         nc.vector.memset(vec_rows[:], 0.0)
         w_raw = consts.tile([P, 2, 4, DO], BF16)
         load(0)
+        nc.sync.dma_start(out=vec_rows[0:1, 0:DO], in_=gcn_m.rearrange("(o c) -> o c", o=1))
+        nc.sync.dma_start(out=vec_rows[0:1, DO : 2 * DO], in_=b_proj.rearrange("(o c) -> o c", o=1))
         for w, w_hbm in ((1, gcn_w), (0, w_proj)):
             nc.sync.dma_start(
                 out=w_raw[:, w, :, :].rearrange("p t c -> p (t c)"),
                 in_=w_hbm.rearrange("(p t) c -> p (t c)", t=4),
             )
-        nc.sync.dma_start(out=vec_rows[0:1, 0:DO], in_=gcn_m.rearrange("(o c) -> o c", o=1))
-        nc.sync.dma_start(out=vec_rows[0:1, DO : 2 * DO], in_=b_proj.rearrange("(o c) -> o c", o=1))
         for k in range(1, LEAD):
             load(k)
 
         ident = consts.tile([P, P], F32)
         masks.make_identity(nc, ident[:])
-        ones = consts.tile([P, P], BF16)
-        nc.vector.memset(ones[:], 1.0)
         ident_bf = consts.tile([P, P], BF16)
         nc.vector.tensor_copy(out=ident_bf[:], in_=ident[:])
         at_ps = ps_a.tile([P, P], BF16, tag="a")
@@ -86,11 +90,6 @@ def tile_gatblock_pa_t_kernel(tc, h_norm, o_attn, a_gcn, w_proj, b_proj, gcn_w, 
         w_grp = consts.tile([P, 2, DO, 4], BF16, align_bytes=64)
         w_codes = consts.tile([P, 2 * DO], U32, align_bytes=64)
         w_scales = consts.tile([P, 2 * DO], U8, align_bytes=64)
-        nc.gpsimd.tensor_scalar(
-            out=w_grp[:, 0, :, :], in0=w_raw[:, 0, :, :].rearrange("p t c -> p c t"),
-            scalar1=1.0, scalar2=0.0, op0=MULT, op1=ADD,
-        )
-
         def quantise_weight(w):
             cols = slice(DO * w, DO * w + DO)
             nc.vector.quantize_mx(
@@ -111,23 +110,24 @@ def tile_gatblock_pa_t_kernel(tc, h_norm, o_attn, a_gcn, w_proj, b_proj, gcn_w, 
         def rows(vec, n):
             return vec[:].unsqueeze(1).to_broadcast([P, n, DO])
 
-        def new_grp(i):
-            grp = work.tile([P, TMAX * P * 8], BF16, align_bytes=64)
-            grp_tiles[i] = grp
+        def grp_of(i):
+            if i not in grp_tiles:
+                grp = work.tile([P, TMAX * P * 8], BF16, align_bytes=64)
+                grp_tiles[i] = grp
+            return grp_tiles[i]
 
         def transposes(i, j0):
             n = SIZES[i]
-            if j0 == 0:
-                new_grp(i)
             nj = min(2, n - j0)
             o_words = o_tiles[i][:].bitcast(F32)
-            go_words = grp_tiles[i][:, 0 : n * P * 4].bitcast(F32).rearrange("p (j r u) -> p j r u", j=n, u=2)
+            go_words = grp_of(i)[:, 0 : n * P * 4].bitcast(F32).rearrange("p (j r u) -> p j r u", j=n, u=2)
             xt = ps_a.tile([P, 2, 2, P], F32, tag="a")
             for jj in range(nj):
                 for u in range(2):
                     c0 = 256 * (j0 + jj)
                     nc.tensor.transpose(xt[:, jj, u, :], o_words[:, c0 + u : c0 + 256 : 2], ident[:])
-            nc.scalar.copy(out=go_words[:, j0 : j0 + nj, :, :], in_=xt[:, 0:nj, :, :].rearrange("p j u r -> p j r u"))
+            copy = nc.vector.tensor_copy if (i, j0) == (1, 2) else nc.scalar.copy
+            copy(out=go_words[:, j0 : j0 + nj, :, :], in_=xt[:, 0:nj, :, :].rearrange("p j u r -> p j r u"))
 
         def mix(i, b):
             n = SIZES[i]
@@ -135,7 +135,7 @@ def tile_gatblock_pa_t_kernel(tc, h_norm, o_attn, a_gcn, w_proj, b_proj, gcn_w, 
             ag = ps_a.tile([P, 4, P], F32, tag="a")
             for t in range(4):
                 nc.tensor.matmul(ag[:, t, :], lhsT=h_tiles[i][:, b, t:D:4], rhs=a_t[:], start=True, stop=True)
-            gg = grp_tiles[i][:, n * P * 4 : n * P * 8].rearrange("p (j r t) -> p j r t", j=n, t=4)
+            gg = grp_of(i)[:, n * P * 4 : n * P * 8].rearrange("p (j r t) -> p j r t", j=n, t=4)
             copy = nc.vector.tensor_copy if i == 0 and b % 2 == 1 else nc.scalar.copy
             copy(out=gg[:, :, r * b : r * b + r, :], in_=ag[:].rearrange("p t (r j) -> p j r t", j=n))
 
@@ -195,7 +195,7 @@ def tile_gatblock_pa_t_kernel(tc, h_norm, o_attn, a_gcn, w_proj, b_proj, gcn_w, 
         def add_bias(i):
             n = SIZES[i]
             res = res_tiles[i][:, 0:n, :]
-            eng = nc.vector if i == NBLK - 1 else nc.gpsimd
+            eng = nc.vector if i >= NBLK - 2 else nc.gpsimd
             eng.tensor_tensor(out=res, in0=res, in1=rows(b_bc, n), op=ADD)
 
         def store(i):
@@ -212,15 +212,19 @@ def tile_gatblock_pa_t_kernel(tc, h_norm, o_attn, a_gcn, w_proj, b_proj, gcn_w, 
         fill, ends, leads = [], [], []
         for i in range(NBLK):
             n = SIZES[i]
-            own = [("t", i, j) for j in range(0, n, 2)] + [("m", i, b) for b in range(n)]
+            own = [("t", i, j) for j in range(0, n, 2)]
+            mixes = [("m", i, b) for b in range(n)]
+            own = mixes + own if i < 2 else own + mixes
             leads.append(len(fill) + (2 * len(own) + 2) // 3)
             fill += own
             ends.append(len(fill))
 
         def upto(w):
+            if w < 0:
+                return ends[0]
             if w + 2 >= NBLK:
                 return len(fill)
-            return max(leads[w + 2] if w + 2 >= 0 else 0, ends[w + 1] if w + 1 >= 0 else 0)
+            return leads[w + 2]
 
         def run_fill(items):
             for kind, i, x in items:
@@ -229,41 +233,48 @@ def tile_gatblock_pa_t_kernel(tc, h_norm, o_attn, a_gcn, w_proj, b_proj, gcn_w, 
                 else:
                     mix(i, x)
 
-        for w in range(-2, NBLK + 1):
-            todo = fill[(upto(w - 1) if w > -2 else 0) : upto(w)]
+        for w in range(-1, NBLK + 1):
+            todo = fill[(upto(w - 1) if w > -1 else 0) : upto(w)]
+            before = 4 if w == 0 else 1
+            if w == 0:
+                for x in (1, 0):
+                    nc.vector.tensor_copy(out=w_grp[:, x, :, :], in_=w_raw[:, x, :, :].rearrange("p t c -> p c t"))
             if live(w):
                 quantise(w)
             if w == 0:
-                nc.vector.tensor_copy(out=w_grp[:, 1, :, :], in_=w_raw[:, 1, :, :].rearrange("p t c -> p c t"))
-                quantise_weight(1)
-                quantise_weight(0)
-            if live(w - 2):
+                for x in (1, 0):
+                    quantise_weight(x)
+            if live(w - 2) and w < NBLK:
                 store(w - 2)
-            run_fill(todo[:1])
+            run_fill(todo[:before])
+            if w == 0:
+                spread_vectors()
             if live(w):
                 mx_passes(w, 1, 0)
-            run_fill(todo[1:-1])
-            if w == -1:
-                spread_vectors()
+            if w == 0:
+                scale_g(0, 0)
+            last = len(todo) if w + 3 >= NBLK else -1
+            run_fill(todo[before:last])
             if live(w - 1):
                 add_o(w - 1, 0)
-            if live(w - 1) and halves(w - 1) == 1:
-                add_bias(w - 1)
+            if w == NBLK:
+                for i in (NBLK - 2, NBLK - 1):
+                    add_bias(i)
+                    store(i)
             if live(w):
                 mx_passes(w, 0, 0)
             if live(w - 1) and halves(w - 1) == 2:
                 scale_g(w - 1, 1)
             if live(w) and halves(w) == 2:
                 mx_passes(w, 1, 1)
-            if live(w):
+            if w > 0 and live(w):
                 scale_g(w, 0)
             if live(w - 1) and halves(w - 1) == 2:
                 add_o(w - 1, 1)
                 add_bias(w - 1)
             if live(w) and halves(w) == 2:
                 mx_passes(w, 0, 1)
-            if len(todo) > 1:
-                run_fill(todo[-1:])
-            if live(w + 2 + LEAD):
-                load(w + 2 + LEAD)
-        store(NBLK - 1)
+            if len(todo) > before:
+                run_fill(todo[last:])
+            if live(w + 1 + LEAD):
+                load(w + 1 + LEAD)

@@ -17,7 +17,7 @@ TMAX = 4
 SIZES = (4,) * 15 + (2, 2)
 STARTS = tuple(sum(SIZES[:i]) for i in range(len(SIZES)))
 NBLK = len(SIZES)
-LEAD = 10
+LEAD = 11
 WARM = 10
 FLOPS = 2 * 2 * B * N * D * DO + 2 * B * N * N * D
 
@@ -36,26 +36,32 @@ def tile_gatblock_pa_t_kernel(tc, h_norm, o_attn, a_gcn, w_proj, b_proj, gcn_w, 
         o_tiles, h_tiles, grp_tiles, code_tiles, scale_tiles = {}, {}, {}, {}, {}
         acc_tiles, res_tiles = {}, {}
 
-        def load(k):
+        def load_h(k, pieces=1):
             s0, n = STARTS[k], SIZES[k]
-            o_sb = consts.tile([P, n * D], BF16, name="o%d" % k)
             h_sb = consts.tile([P, n, D], BF16, name="h%d" % k)
-            o_tiles[k] = o_sb
             h_tiles[k] = h_sb
-            o_rows = o_attn[s0 : s0 + n, :, :].flatten_outer_dims()
-            pieces = 2 if k == 0 else 1
             c = n // pieces
             for q in range(pieces):
                 nc.sync.dma_start(
                     out=h_sb[:, c * q : c * (q + 1), :],
                     in_=h_norm[s0 + c * q : s0 + c * (q + 1), :, :].rearrange("b n d -> n b d"),
                 )
+
+        def load_o(k, pieces=1):
+            s0, n = STARTS[k], SIZES[k]
+            o_sb = consts.tile([P, n * D], BF16, name="o%d" % k)
+            o_tiles[k] = o_sb
+            o_rows = o_attn[s0 : s0 + n, :, :].flatten_outer_dims()
             c = n * D // pieces
             for q in range(pieces):
                 nc.sync.dma_start(
                     out=o_sb[:, c * q : c * (q + 1)],
                     in_=o_rows.rearrange("(p j) d -> p (j d)", p=P)[:, c * q : c * (q + 1)],
                 )
+
+        def load(k):
+            load_h(k)
+            load_o(k)
 
         ones = consts.tile([P, P], BF16)
         nc.vector.memset(ones[:], 1.0)
@@ -67,14 +73,15 @@ def tile_gatblock_pa_t_kernel(tc, h_norm, o_attn, a_gcn, w_proj, b_proj, gcn_w, 
         vec_rows = consts.tile([P, 2 * DO], BF16)
         nc.vector.memset(vec_rows[:], 0.0)
         w_raw = consts.tile([P, 2, 4, DO], BF16)
-        load(0)
-        nc.sync.dma_start(out=vec_rows[0:1, 0:DO], in_=gcn_m.rearrange("(o c) -> o c", o=1))
-        nc.sync.dma_start(out=vec_rows[0:1, DO : 2 * DO], in_=b_proj.rearrange("(o c) -> o c", o=1))
+        load_h(0, 2)
         for w, w_hbm in ((1, gcn_w), (0, w_proj)):
             nc.sync.dma_start(
                 out=w_raw[:, w, :, :].rearrange("p t c -> p (t c)"),
                 in_=w_hbm.rearrange("(p t) c -> p (t c)", t=4),
             )
+        load_o(0, 2)
+        nc.sync.dma_start(out=vec_rows[0:1, 0:DO], in_=gcn_m.rearrange("(o c) -> o c", o=1))
+        nc.sync.dma_start(out=vec_rows[0:1, DO : 2 * DO], in_=b_proj.rearrange("(o c) -> o c", o=1))
         for k in range(1, LEAD):
             load(k)
 
@@ -99,7 +106,7 @@ def tile_gatblock_pa_t_kernel(tc, h_norm, o_attn, a_gcn, w_proj, b_proj, gcn_w, 
             )
 
         m_bc = consts.tile([P, DO], F32)
-        b_bc = consts.tile([P, DO], F32)
+        b_bc = consts.tile([P, DO], BF16)
 
         def spread_vectors():
             vec_ps = ps_a.tile([P, 2 * DO], F32, tag="a")
@@ -233,22 +240,21 @@ def tile_gatblock_pa_t_kernel(tc, h_norm, o_attn, a_gcn, w_proj, b_proj, gcn_w, 
                 else:
                     mix(i, x)
 
-        for w in range(-1, NBLK + 1):
-            todo = fill[(upto(w - 1) if w > -1 else 0) : upto(w)]
+        run_fill(fill[: ends[0]])
+        spread_vectors()
+        for w in range(NBLK + 1):
+            todo = fill[upto(w - 1) : upto(w)]
             before = 4 if w == 0 else 1
             if w == 0:
                 for x in (1, 0):
                     nc.vector.tensor_copy(out=w_grp[:, x, :, :], in_=w_raw[:, x, :, :].rearrange("p t c -> p c t"))
-            if live(w):
-                quantise(w)
-            if w == 0:
                 for x in (1, 0):
                     quantise_weight(x)
+            if live(w):
+                quantise(w)
             if live(w - 2) and w < NBLK:
                 store(w - 2)
             run_fill(todo[:before])
-            if w == 0:
-                spread_vectors()
             if live(w):
                 mx_passes(w, 1, 0)
             if w == 0:
@@ -258,9 +264,10 @@ def tile_gatblock_pa_t_kernel(tc, h_norm, o_attn, a_gcn, w_proj, b_proj, gcn_w, 
             if live(w - 1):
                 add_o(w - 1, 0)
             if w == NBLK:
-                for i in (NBLK - 2, NBLK - 1):
-                    add_bias(i)
-                    store(i)
+                add_bias(NBLK - 2)
+                store(NBLK - 2)
+                add_bias(NBLK - 1)
+                store(NBLK - 1)
             if live(w):
                 mx_passes(w, 0, 0)
             if live(w - 1) and halves(w - 1) == 2:
@@ -276,5 +283,5 @@ def tile_gatblock_pa_t_kernel(tc, h_norm, o_attn, a_gcn, w_proj, b_proj, gcn_w, 
                 mx_passes(w, 0, 1)
             if len(todo) > before:
                 run_fill(todo[last:])
-            if live(w + 1 + LEAD):
-                load(w + 1 + LEAD)
+            if live(w + LEAD):
+                load(w + LEAD)

@@ -17,7 +17,7 @@ TMAX = 4
 SIZES = (4,) * 15 + (2, 2)
 STARTS = tuple(sum(SIZES[:i]) for i in range(len(SIZES)))
 NBLK = len(SIZES)
-LEAD = 11
+LEAD = 10
 WARM = 10
 FLOPS = 2 * 2 * B * N * D * DO + 2 * B * N * N * D
 
@@ -28,7 +28,8 @@ def tile_gatblock_pa_t_kernel(tc, h_norm, o_attn, a_gcn, w_proj, b_proj, gcn_w, 
     with ExitStack() as ctx:
         consts = ctx.enter_context(tc.tile_pool(name="consts", bufs=1))
         work = ctx.enter_context(tc.tile_pool(name="work", bufs=3))
-        outs = ctx.enter_context(tc.tile_pool(name="outs", bufs=8))
+        inputs = ctx.enter_context(tc.tile_pool(name="inputs", bufs=LEAD))
+        outs = ctx.enter_context(tc.tile_pool(name="outs", bufs=NBLK))
         ps_a = ctx.enter_context(tc.psum_pool(name="ps_a", bufs=4))
         ps_m = ctx.enter_context(tc.psum_pool(name="ps_m", bufs=1))
         ctx.enter_context(tc.manual_schedule())
@@ -38,7 +39,7 @@ def tile_gatblock_pa_t_kernel(tc, h_norm, o_attn, a_gcn, w_proj, b_proj, gcn_w, 
 
         def load_h(k, pieces=1):
             s0, n = STARTS[k], SIZES[k]
-            h_sb = consts.tile([P, n, D], BF16, name="h%d" % k)
+            h_sb = inputs.tile([P, n, D], BF16)
             h_tiles[k] = h_sb
             c = n // pieces
             for q in range(pieces):
@@ -49,7 +50,7 @@ def tile_gatblock_pa_t_kernel(tc, h_norm, o_attn, a_gcn, w_proj, b_proj, gcn_w, 
 
         def load_o(k, pieces=1):
             s0, n = STARTS[k], SIZES[k]
-            o_sb = consts.tile([P, n * D], BF16, name="o%d" % k)
+            o_sb = inputs.tile([P, n * D], BF16)
             o_tiles[k] = o_sb
             o_rows = o_attn[s0 : s0 + n, :, :].flatten_outer_dims()
             c = n * D // pieces
@@ -199,19 +200,15 @@ def tile_gatblock_pa_t_kernel(tc, h_norm, o_attn, a_gcn, w_proj, b_proj, gcn_w, 
             part = res_tiles[i][:, 2 * half : 2 * half + n, :]
             nc.vector.tensor_tensor(out=part, in0=acc_tiles[(i, 0, half)][:, 0:n, :], in1=part, op=ADD)
 
-        def add_bias(i):
-            n = SIZES[i]
-            res = res_tiles[i][:, 0:n, :]
-            eng = nc.vector if i >= NBLK - 2 else nc.gpsimd
-            eng.tensor_tensor(out=res, in0=res, in1=rows(b_bc, n), op=ADD)
+        def add_bias(eng, i, j0, j1):
+            res = res_tiles[i][:, j0:j1, :]
+            eng.tensor_tensor(out=res, in0=res, in1=rows(b_bc, j1 - j0), op=ADD)
 
-        def store(i):
+        def store(i, j0=0, j1=None):
             s0, n = STARTS[i], SIZES[i]
-            out_rows = out[s0 : s0 + n, :, :].flatten_outer_dims()
-            nc.sync.dma_start(
-                out=out_rows.rearrange("(p j) c -> p (j c)", p=P),
-                in_=res_tiles[i][:, 0:n, :].rearrange("p j c -> p (j c)"),
-            )
+            j1 = n if j1 is None else j1
+            out_rows = out[s0 : s0 + n, :, :].flatten_outer_dims().rearrange("(p j) c -> p j c", p=P)
+            nc.sync.dma_start(out=out_rows[:, j0:j1, :], in_=res_tiles[i][:, j0:j1, :])
 
         def live(i):
             return 0 <= i < NBLK
@@ -252,8 +249,11 @@ def tile_gatblock_pa_t_kernel(tc, h_norm, o_attn, a_gcn, w_proj, b_proj, gcn_w, 
                     quantise_weight(x)
             if live(w):
                 quantise(w)
-            if live(w - 2) and w < NBLK:
+            if live(w - 2) and w < NBLK - 1:
                 store(w - 2)
+            if w == NBLK - 1:
+                store(w - 2, 0, 2)
+                store(w - 2, 2, 4)
             run_fill(todo[:before])
             if live(w):
                 mx_passes(w, 1, 0)
@@ -261,13 +261,17 @@ def tile_gatblock_pa_t_kernel(tc, h_norm, o_attn, a_gcn, w_proj, b_proj, gcn_w, 
                 scale_g(0, 0)
             last = len(todo) if w + 3 >= NBLK else -1
             run_fill(todo[before:last])
+            if w == NBLK:
+                add_bias(nc.vector, NBLK - 2, 0, 2)
+                store(NBLK - 2)
             if live(w - 1):
                 add_o(w - 1, 0)
+            if w == NBLK - 2:
+                add_bias(nc.gpsimd, w - 1, 0, 2)
             if w == NBLK:
-                add_bias(NBLK - 2)
-                store(NBLK - 2)
-                add_bias(NBLK - 1)
-                store(NBLK - 1)
+                for j in range(2):
+                    add_bias(nc.vector, NBLK - 1, j, j + 1)
+                    store(NBLK - 1, j, j + 1)
             if live(w):
                 mx_passes(w, 0, 0)
             if live(w - 1) and halves(w - 1) == 2:
@@ -278,7 +282,7 @@ def tile_gatblock_pa_t_kernel(tc, h_norm, o_attn, a_gcn, w_proj, b_proj, gcn_w, 
                 scale_g(w, 0)
             if live(w - 1) and halves(w - 1) == 2:
                 add_o(w - 1, 1)
-                add_bias(w - 1)
+                add_bias(nc.gpsimd, w - 1, 2 if w == NBLK - 2 else 0, 4)
             if live(w) and halves(w) == 2:
                 mx_passes(w, 0, 1)
             if len(todo) > before:

@@ -255,6 +255,8 @@ def tile_gatblock_pa_t_kernel(tc, h_norm, o_attn, a_gcn, w_proj, b_proj, gcn_w, 
                 store(w - 2, 0, 2)
                 store(w - 2, 2, 4)
             run_fill(todo[:before])
+            if live(w - 1) and halves(w - 1) == 2:
+                mx_passes(w - 1, 0, 1)
             if live(w):
                 mx_passes(w, 1, 0)
             if w == 0:
@@ -283,8 +285,6 @@ def tile_gatblock_pa_t_kernel(tc, h_norm, o_attn, a_gcn, w_proj, b_proj, gcn_w, 
             if live(w - 1) and halves(w - 1) == 2:
                 add_o(w - 1, 1)
                 add_bias(nc.gpsimd, w - 1, 2 if w == NBLK - 2 else 0, 4)
-            if live(w) and halves(w) == 2:
-                mx_passes(w, 0, 1)
             if len(todo) > before:
                 run_fill(todo[last:])
             if live(w + LEAD):

from contextlib import ExitStack

import concourse.masks as masks
import concourse.mybir as mybir

F32 = mybir.dt.float32
BF16 = mybir.dt.bfloat16
U32 = mybir.dt.uint32
U8 = mybir.dt.uint8
FP8X4 = mybir.dt.float8_e4m3fn_x4
MULT = mybir.AluOpType.mult
ADD = mybir.AluOpType.add

P = 128
B, N, D, DO = 64, 128, 512, 256
TMAX = 4
SIZES = (4,) * 15 + (2, 2)
STARTS = tuple(sum(SIZES[:i]) for i in range(len(SIZES)))
NBLK = len(SIZES)
LEAD = 10
WARM = 10
FLOPS = 2 * 2 * B * N * D * DO + 2 * B * N * N * D


def tile_gatblock_pa_t_kernel(tc, h_norm, o_attn, a_gcn, w_proj, b_proj, gcn_w, gcn_m, out):
    nc = tc.nc

    with ExitStack() as ctx:
        consts = ctx.enter_context(tc.tile_pool(name="consts", bufs=1))
        work = ctx.enter_context(tc.tile_pool(name="work", bufs=3))
        inputs = ctx.enter_context(tc.tile_pool(name="inputs", bufs=LEAD))
        outs = ctx.enter_context(tc.tile_pool(name="outs", bufs=NBLK))
        ps_a = ctx.enter_context(tc.psum_pool(name="ps_a", bufs=4))
        ps_m = ctx.enter_context(tc.psum_pool(name="ps_m", bufs=1))
        ctx.enter_context(tc.manual_schedule())

        o_tiles, h_tiles, grp_tiles, code_tiles, scale_tiles = {}, {}, {}, {}, {}
        acc_tiles, res_tiles = {}, {}

        def load_h(k, pieces=1):
            s0, n = STARTS[k], SIZES[k]
            h_sb = inputs.tile([P, n, D], BF16)
            h_tiles[k] = h_sb
            c = n // pieces
            for q in range(pieces):
                nc.sync.dma_start(
                    out=h_sb[:, c * q : c * (q + 1), :],
                    in_=h_norm[s0 + c * q : s0 + c * (q + 1), :, :].rearrange("b n d -> n b d"),
                )

        def load_o(k, pieces=1):
            s0, n = STARTS[k], SIZES[k]
            o_sb = inputs.tile([P, n * D], BF16)
            o_tiles[k] = o_sb
            o_rows = o_attn[s0 : s0 + n, :, :].flatten_outer_dims()
            c = n * D // pieces
            for q in range(pieces):
                nc.sync.dma_start(
                    out=o_sb[:, c * q : c * (q + 1)],
                    in_=o_rows.rearrange("(p j) d -> p (j d)", p=P)[:, c * q : c * (q + 1)],
                )

        def load(k):
            load_h(k)
            load_o(k)

        ones = consts.tile([P, P], BF16)
        nc.vector.memset(ones[:], 1.0)
        warm_ps = ps_a.tile([P, P], F32, tag="a")
        for x in range(WARM):
            nc.tensor.matmul(warm_ps[:], lhsT=ones[:], rhs=ones[:], start=True, stop=True)
        a_sb = consts.tile([P, P], BF16)
        nc.sync.dma_start(out=a_sb[:], in_=a_gcn)
        vec_rows = consts.tile([P, 2 * DO], BF16)
        nc.vector.memset(vec_rows[:], 0.0)
        w_raw = consts.tile([P, 2, 4, DO], BF16)
        load_h(0, 2)
        for w, w_hbm in ((1, gcn_w), (0, w_proj)):
            nc.sync.dma_start(
                out=w_raw[:, w, :, :].rearrange("p t c -> p (t c)"),
                in_=w_hbm.rearrange("(p t) c -> p (t c)", t=4),
            )
        load_o(0, 2)
        nc.sync.dma_start(out=vec_rows[0:1, 0:DO], in_=gcn_m.rearrange("(o c) -> o c", o=1))
        nc.sync.dma_start(out=vec_rows[0:1, DO : 2 * DO], in_=b_proj.rearrange("(o c) -> o c", o=1))
        for k in range(1, LEAD):
            load(k)

        ident = consts.tile([P, P], F32)
        masks.make_identity(nc, ident[:])
        ident_bf = consts.tile([P, P], BF16)
        nc.vector.tensor_copy(out=ident_bf[:], in_=ident[:])
        at_ps = ps_a.tile([P, P], BF16, tag="a")
        nc.tensor.transpose(at_ps[:], a_sb[:], ident_bf[:])
        a_t = consts.tile([P, P], BF16)
        nc.vector.tensor_copy(out=a_t[:], in_=at_ps[:])

        w_grp = consts.tile([P, 2, DO, 4], BF16, align_bytes=64)
        w_codes = consts.tile([P, 2 * DO], U32, align_bytes=64)
        w_scales = consts.tile([P, 2 * DO], U8, align_bytes=64)
        def quantise_weight(w):
            cols = slice(DO * w, DO * w + DO)
            nc.vector.quantize_mx(
                out=w_codes[:, cols].bitcast(FP8X4),
                scales=w_scales[:, cols],
                in_=w_grp[:, w, :, :].rearrange("p c t -> p (c t)"),
            )

        m_bc = consts.tile([P, DO], F32)
        b_bc = consts.tile([P, DO], BF16)

        def spread_vectors():
            vec_ps = ps_a.tile([P, 2 * DO], F32, tag="a")
            nc.tensor.matmul(vec_ps[:], lhsT=ones[:], rhs=vec_rows[:], start=True, stop=True)
            nc.scalar.copy(out=m_bc[:], in_=vec_ps[:, 0:DO])
            nc.scalar.copy(out=b_bc[:], in_=vec_ps[:, DO : 2 * DO])

        def rows(vec, n):
            return vec[:].unsqueeze(1).to_broadcast([P, n, DO])

        def grp_of(i):
            if i not in grp_tiles:
                grp = work.tile([P, TMAX * P * 8], BF16, align_bytes=64)
                grp_tiles[i] = grp
            return grp_tiles[i]

        def transposes(i, j0):
            n = SIZES[i]
            nj = min(2, n - j0)
            o_words = o_tiles[i][:].bitcast(F32)
            go_words = grp_of(i)[:, 0 : n * P * 4].bitcast(F32).rearrange("p (j r u) -> p j r u", j=n, u=2)
            xt = ps_a.tile([P, 2, 2, P], F32, tag="a")
            for jj in range(nj):
                for u in range(2):
                    c0 = 256 * (j0 + jj)
                    nc.tensor.transpose(xt[:, jj, u, :], o_words[:, c0 + u : c0 + 256 : 2], ident[:])
            copy = nc.vector.tensor_copy if (i, j0) == (1, 2) else nc.scalar.copy
            copy(out=go_words[:, j0 : j0 + nj, :, :], in_=xt[:, 0:nj, :, :].rearrange("p j u r -> p j r u"))

        def mix(i, b):
            n = SIZES[i]
            r = P // n
            ag = ps_a.tile([P, 4, P], F32, tag="a")
            for t in range(4):
                nc.tensor.matmul(ag[:, t, :], lhsT=h_tiles[i][:, b, t:D:4], rhs=a_t[:], start=True, stop=True)
            gg = grp_of(i)[:, n * P * 4 : n * P * 8].rearrange("p (j r t) -> p j r t", j=n, t=4)
            copy = nc.vector.tensor_copy if i == 0 and b % 2 == 1 else nc.scalar.copy
            copy(out=gg[:, :, r * b : r * b + r, :], in_=ag[:].rearrange("p t (r j) -> p j r t", j=n))

        def quantise(i):
            n = SIZES[i]
            codes = work.tile([P, 2 * TMAX * P], U32, align_bytes=64)
            scales = work.tile([P, 2 * TMAX * P], U8, align_bytes=64)
            nc.vector.quantize_mx(
                out=codes[:, 0 : 2 * n * P].bitcast(FP8X4),
                scales=scales[:, 0 : 2 * n * P],
                in_=grp_tiles[i][:, 0 : n * P * 8],
            )
            code_tiles[i] = codes
            scale_tiles[i] = scales

        def halves(i):
            return (SIZES[i] + 1) // 2

        single = {}
        for i in range(NBLK):
            single[i] = 1 - single[i - 1] if i > 0 and halves(i - 1) == 1 else 0

        def bank(i, half):
            return half if halves(i) == 2 else single[i]

        def width(i):
            return min(2, SIZES[i])

        def mx_passes(i, which, half):
            acc = ps_m.tile([P, 2, DO], F32, tag="m%d%d" % (which, bank(i, half)))
            acc_tiles[(i, which, half)] = acc
            for jj in range(width(i)):
                c0 = SIZES[i] * P * which + P * (2 * half + jj)
                nc.tensor.matmul_mx(
                    out=acc[:, jj, :],
                    lhsT=code_tiles[i][:, c0 : c0 + P].bitcast(FP8X4),
                    lhsT_scale=scale_tiles[i][:, c0 : c0 + P],
                    rhs=w_codes[:, DO * which : DO * which + DO].bitcast(FP8X4),
                    rhs_scale=w_scales[:, DO * which : DO * which + DO],
                    start=True,
                    stop=True,
                )

        def scale_g(i, half):
            if half == 0:
                res = outs.tile([P, TMAX, DO], F32)
                res_tiles[i] = res
            n = width(i)
            part = res_tiles[i][:, 2 * half : 2 * half + n, :]
            nc.vector.tensor_tensor(out=part, in0=acc_tiles[(i, 1, half)][:, 0:n, :], in1=rows(m_bc, n), op=MULT)

        def add_o(i, half):
            n = width(i)
            part = res_tiles[i][:, 2 * half : 2 * half + n, :]
            nc.vector.tensor_tensor(out=part, in0=acc_tiles[(i, 0, half)][:, 0:n, :], in1=part, op=ADD)

        def add_bias(eng, i, j0, j1):
            res = res_tiles[i][:, j0:j1, :]
            eng.tensor_tensor(out=res, in0=res, in1=rows(b_bc, j1 - j0), op=ADD)

        def store(i, j0=0, j1=None):
            s0, n = STARTS[i], SIZES[i]
            j1 = n if j1 is None else j1
            out_rows = out[s0 : s0 + n, :, :].flatten_outer_dims().rearrange("(p j) c -> p j c", p=P)
            nc.sync.dma_start(out=out_rows[:, j0:j1, :], in_=res_tiles[i][:, j0:j1, :])

        def live(i):
            return 0 <= i < NBLK

        fill, ends, leads = [], [], []
        for i in range(NBLK):
            n = SIZES[i]
            own = [("t", i, j) for j in range(0, n, 2)]
            mixes = [("m", i, b) for b in range(n)]
            own = mixes + own if i < 2 else own + mixes
            leads.append(len(fill) + (2 * len(own) + 2) // 3)
            fill += own
            ends.append(len(fill))

        def upto(w):
            if w < 0:
                return ends[0]
            if w + 2 >= NBLK:
                return len(fill)
            return leads[w + 2]

        def run_fill(items):
            for kind, i, x in items:
                if kind == "t":
                    transposes(i, x)
                else:
                    mix(i, x)

        run_fill(fill[: ends[0]])
        spread_vectors()
        for w in range(NBLK + 1):
            todo = fill[upto(w - 1) : upto(w)]
            before = 4 if w == 0 else 1
            if w == 0:
                for x in (1, 0):
                    nc.vector.tensor_copy(out=w_grp[:, x, :, :], in_=w_raw[:, x, :, :].rearrange("p t c -> p c t"))
                for x in (1, 0):
                    quantise_weight(x)
            if live(w):
                quantise(w)
            if live(w - 2) and w < NBLK - 1:
                store(w - 2)
            if w == NBLK - 1:
                store(w - 2, 0, 2)
                store(w - 2, 2, 4)
            run_fill(todo[:before])
            if live(w - 1) and halves(w - 1) == 2:
                mx_passes(w - 1, 0, 1)
            if live(w):
                mx_passes(w, 1, 0)
            if w == 0:
                scale_g(0, 0)
            last = len(todo) if w + 3 >= NBLK else -1
            run_fill(todo[before:last])
            if w == NBLK:
                add_bias(nc.vector, NBLK - 2, 0, 2)
                store(NBLK - 2)
            if live(w - 1):
                add_o(w - 1, 0)
            if w == NBLK - 2:
                add_bias(nc.gpsimd, w - 1, 0, 2)
            if w == NBLK:
                for j in range(2):
                    add_bias(nc.vector, NBLK - 1, j, j + 1)
                    store(NBLK - 1, j, j + 1)
            if live(w):
                mx_passes(w, 0, 0)
            if live(w - 1) and halves(w - 1) == 2:
                scale_g(w - 1, 1)
            if live(w) and halves(w) == 2:
                mx_passes(w, 1, 1)
            if w > 0 and live(w):
                scale_g(w, 0)
            if live(w - 1) and halves(w - 1) == 2:
                add_o(w - 1, 1)
                add_bias(nc.gpsimd, w - 1, 2 if w == NBLK - 2 else 0, 4)
            if len(todo) > before:
                run_fill(todo[last:])
            if live(w + LEAD):
                load(w + LEAD)
